import numpy as np
import ml_dtypes


def mxq(x, axis, fmt="e4m3"):
    dtype, down = {"e4m3": (ml_dtypes.float8_e4m3fn, 7), "e5m2": (ml_dtypes.float8_e5m2, 14)}[fmt]
    v = np.moveaxis(np.asarray(x, np.float32).astype(ml_dtypes.bfloat16).astype(np.float64), axis, -1)
    blocks = v.reshape(v.shape[:-1] + (-1, 32))
    amax = np.abs(blocks).max(-1, keepdims=True)
    byte = np.maximum(np.where(amax > 0, np.frexp(amax)[1] - 1 + 127, 0) - down, 1)
    scale = np.exp2(byte - 127.0)
    codes = (blocks / scale).astype(np.float32).astype(dtype).astype(np.float64)
    return np.moveaxis((codes * scale).reshape(v.shape), -1, axis)


WIDE = False


def mx_kscale(k):
    if not WIDE:
        return np.ones(k)
    levels = np.array([10, -10, 5, -5, 0])
    a = np.random.permutation(np.resize(levels, k // 512 * 4)).reshape(k // 512, 4)
    idx = np.arange(k)
    return np.exp2(a[idx // 512, idx % 128 // 32])


BF16 = ml_dtypes.bfloat16


def bf(x):
    return np.asarray(x, np.float32).astype(BF16)


def f64(x):
    return np.asarray(x).astype(np.float64)


B, N, HH, WW, TC, IC, DQK = 3, 256, 32, 32, 1024, 1024, 512
M = HH * WW
AQK = np.sqrt(2.0) / DQK ** 0.25


def setup_inputs():
    s = mx_kscale(TC)
    t = mx_kscale(DQK)
    return {"x1": bf(np.random.standard_normal((B, N, TC)) * s),
            "Wq": bf(np.random.standard_normal((TC, DQK)) * AQK / np.sqrt(TC) / s[:, None] * t),
            "bq": bf(np.random.standard_normal(DQK) * 0.25 * AQK * t),
            "k_img": bf(np.random.standard_normal((B, M, DQK)) * AQK / t),
            "masks": bf(np.random.uniform(size=(B, N, M)) > 0.2)}


def reference(x1, Wq, bq, k_img, masks):
    q = (mxq(f64(x1), 2, "e4m3") @ mxq(f64(Wq), 0, "e4m3")) + f64(bq)
    s = mxq(q, 2, "e4m3") @ mxq(f64(k_img), 2, "e4m3").transpose(0, 2, 1)
    e = np.exp(s - s.max(-1, keepdims=True))
    return e / e.sum(-1, keepdims=True) * f64(masks)

@@ -1,0 +1,337 @@
+from contextlib import ExitStack
+
+import concourse.mybir as mybir
+from concourse.masks import make_identity
+
+F32 = mybir.dt.float32
+BF16 = mybir.dt.bfloat16
+U32 = mybir.dt.uint32
+U8 = mybir.dt.uint8
+FP8X4 = mybir.dt.float8_e4m3fn_x4
+ALU = mybir.AluOpType
+ACT = mybir.ActivationFunctionType
+AX = mybir.AxisListType
+
+P = 128
+B, N, TC, DQK, M = 3, 256, 1024, 512, 1024
+NT = 6
+FLOPS = 2 * B * N * TC * DQK + 2 * B * N * M * DQK
+
+PIN = False
+
+
+def tile_text2imgca_pa_kernel(tc, x1, Wq, bq, k_img, masks, out):
+    nc = tc.nc
+    with ExitStack() as ctx:
+        keep = ctx.enter_context(tc.tile_pool(name="keep", bufs=1))
+        stage = ctx.enter_context(tc.tile_pool(name="stage", bufs=3))
+        small = ctx.enter_context(tc.tile_pool(name="small", bufs=4))
+        tpool = ctx.enter_context(tc.psum_pool(name="tpool", bufs=3))
+        qpool = ctx.enter_context(tc.psum_pool(name="qpool", bufs=1))
+        spool = ctx.enter_context(tc.psum_pool(name="spool", bufs=4))
+
+        ident = keep.tile([P, P], F32, name="ident")
+        make_identity(nc, ident[:])
+
+        wraw = keep.tile([P, 4096], BF16, name="wraw")
+        wg = keep.tile([P, 4096], BF16, name="wg", align_bytes=64)
+        wq = keep.tile([P, 2, 512], U32, name="wq", align_bytes=64)
+        ws = keep.tile([P, 2, 512], U8, name="ws", align_bytes=64)
+        xraw = keep.tile([P, B * 2048], BF16, name="xraw")
+        xq = keep.tile([P, NT, 256], U32, name="xq", align_bytes=64)
+        xs = keep.tile([P, NT, 256], U8, name="xs", align_bytes=64)
+        kraw = keep.tile([P, B * 4096], BF16, name="kraw")
+        kq = keep.tile([P, NT, 512], U32, name="kq", align_bytes=64)
+        ks = keep.tile([P, NT, 512], U8, name="ks", align_bytes=64)
+        qq = keep.tile([P, NT, 128], U32, name="qq", align_bytes=64)
+        qs = keep.tile([P, NT, 128], U8, name="qs", align_bytes=64)
+        mraw = keep.tile([P, B * 2048], BF16, name="mraw")
+        bias = keep.tile([P, 4], BF16, name="bias")
+        warm = keep.tile([P, 1], F32, name="warm")
+        warm2 = keep.tile([P, 1], F32, name="warm2")
+
+        if PIN:
+            ctx.enter_context(tc.manual_schedule())
+
+        with nc.allow_non_contiguous_dma(reason="bias: 256 pieces of 4 bytes, once"):
+            nc.scalar.dma_start(
+                out=bias[:].rearrange("p (u e) -> p u e", u=2),
+                in_=bq.rearrange("(u p e) -> p u e", u=2, p=P, e=2),
+            )
+        nc.vector.memset(warm[:], 0.0)
+        nc.scalar.activation(out=warm2[:], in_=warm[:], func=ACT.Exp)
+
+        def load_w(g):
+            nc.sync.dma_start(
+                out=wraw[:, g * 2048:(g + 1) * 2048].rearrange("p (u f) -> p u f", u=2),
+                in_=Wq[g * 512:(g + 1) * 512, :].rearrange("(u q e) c -> q u (e c)", u=2, q=P, e=2),
+            )
+
+        def load_x(b):
+            nc.sync.dma_start(
+                out=xraw[:, b * 2048:(b + 1) * 2048],
+                in_=x1[b].rearrange("(r a) k -> r (a k)", a=2),
+            )
+
+        def load_k(b, c):
+            nc.sync.dma_start(
+                out=kraw[:, b * 4096 + c * 2048: b * 4096 + (c + 1) * 2048].rearrange("p (c f) -> p c f", c=2),
+                in_=k_img[b, c * 512:(c + 1) * 512, :].rearrange("(c r a) d -> r c (a d)", c=2, r=P, a=2),
+            )
+
+        def load_m(b):
+            nc.sync.dma_start(
+                out=mraw[:, b * 2048:(b + 1) * 2048],
+                in_=masks[b].rearrange("(r a) m -> r (a m)", a=2),
+            )
+
+        load_w(0)
+        load_w(1)
+        load_x(0)
+        load_k(0, 0)
+        load_k(0, 1)
+        load_x(1)
+        load_k(1, 0)
+        load_k(1, 1)
+        load_m(0)
+        load_x(2)
+        load_k(2, 0)
+        load_k(2, 1)
+        load_m(1)
+        load_m(2)
+
+        xw = xraw[:].bitcast(F32)
+        kw = kraw[:].bitcast(F32)
+
+        wgv = wg[:].rearrange("p (g u e m j) -> p g u e m j", g=2, u=2, e=2, m=P, j=4)
+        wrv = wraw[:].rearrange("p (g j u m e) -> p g j u m e", g=2, j=4, u=2, m=P, e=2)
+
+        def wreg(g, e, eng):
+            dst = wgv[:, g, :, e]
+            srcv = wrv[:, g, :, :, :, e].rearrange("p j u m -> p u m j")
+            if eng == "v":
+                nc.vector.tensor_copy(out=dst, in_=srcv)
+            else:
+                nc.scalar.copy(out=dst, in_=srcv)
+
+        def qz_w(g):
+            nc.vector.quantize_mx(
+                out=wq[:, g, :].bitcast(FP8X4), scales=ws[:, g, :],
+                in_=wg[:, g * 2048:(g + 1) * 2048],
+            )
+
+        live = {}
+
+        def t_x(i):
+            if i >= NT:
+                return
+            tp = tpool.tile([P, 512], F32, name="tp")
+            for s in range(4):
+                nc.tensor.transpose(
+                    out=tp[:, s * P:(s + 1) * P],
+                    in_=xw[:, i * 512 + s * P: i * 512 + (s + 1) * P],
+                    identity=ident[:],
+                )
+            live[("tx", i)] = tp
+
+        def copy_out(eng, dst, srcv):
+            if eng == "v":
+                nc.vector.tensor_copy(out=dst, in_=srcv)
+            else:
+                nc.scalar.copy(out=dst, in_=srcv)
+
+        def e_x(i, eng="s"):
+            if i >= NT:
+                return
+            tp = live.pop(("tx", i))
+            xg = stage.tile([P, 512], F32, name="xg", align_bytes=64)
+            copy_out(
+                eng,
+                xg[:].rearrange("p (g r u) -> p g r u", g=2, r=P, u=2),
+                tp[:].rearrange("p (g u r) -> p g r u", g=2, u=2, r=P),
+            )
+            live[("xg", i)] = xg
+
+        def qz_x(i):
+            if i >= NT:
+                return
+            xg = live.pop(("xg", i))
+            nc.vector.quantize_mx(
+                out=xq[:, i, :].bitcast(FP8X4), scales=xs[:, i, :], in_=xg[:].bitcast(BF16),
+            )
+
+        def t_k(i):
+            if i >= NT:
+                return
+            for h in range(2):
+                tp = tpool.tile([P, 512], F32, name="tp")
+                for s in range(4):
+                    base = i * 1024 + h * 512 + s * P
+                    nc.tensor.transpose(
+                        out=tp[:, s * P:(s + 1) * P], in_=kw[:, base: base + P], identity=ident[:],
+                    )
+                live[("tk", i, h)] = tp
+
+        def e_k(i, engs=("s", "s")):
+            if i >= NT:
+                return
+            kg = stage.tile([P, 1024], F32, name="kg", align_bytes=64)
+            for h in range(2):
+                tp = live.pop(("tk", i, h))
+                copy_out(
+                    engs[h],
+                    kg[:, h * 512:(h + 1) * 512].rearrange("p (r s) -> p r s", s=4),
+                    tp[:].rearrange("p (s r) -> p r s", s=4),
+                )
+            live[("kg", i)] = kg
+
+        def qz_k(i):
+            if i >= NT:
+                return
+            kg = live.pop(("kg", i))
+            nc.vector.quantize_mx(
+                out=kq[:, i, :].bitcast(FP8X4), scales=ks[:, i, :], in_=kg[:].bitcast(BF16),
+            )
+
+        def m1(i):
+            if i >= NT:
+                return
+            qp = qpool.tile([P, 512], F32, name="qp")
+            for t in range(4):
+                for g in range(2):
+                    nc.tensor.matmul_mx(
+                        out=qp[:, t * P:(t + 1) * P],
+                        lhsT=wq[:, g, t * P:(t + 1) * P].bitcast(FP8X4),
+                        lhsT_scale=ws[:, g, t * P:(t + 1) * P],
+                        rhs=xq[:, i, g * P:(g + 1) * P].bitcast(FP8X4),
+                        rhs_scale=xs[:, i, g * P:(g + 1) * P],
+                        start=(g == 0), stop=(g == 1),
+                    )
+            live[("qp", i)] = qp
+
+        def badd(i):
+            if i >= NT:
+                return
+            qp = live.pop(("qp", i))
+            qg = stage.tile([P, 512], BF16, name="qg", align_bytes=64)
+            nc.vector.tensor_tensor(
+                out=qg[:].rearrange("p (r t) -> p r t", t=4),
+                in0=qp[:].rearrange("p (t r) -> p r t", t=4),
+                in1=bias[:].unsqueeze(1).to_broadcast([P, P, 4]),
+                op=ALU.add,
+            )
+            live[("qg", i)] = qg
+
+        def qz_q(i):
+            if i >= NT:
+                return
+            qg = live.pop(("qg", i))
+            nc.vector.quantize_mx(
+                out=qq[:, i, :].bitcast(FP8X4), scales=qs[:, i, :], in_=qg[:],
+            )
+
+        def m2(i):
+            if i >= NT:
+                return
+            b = i // 2
+            for c in range(2):
+                sp = spool.tile([P, 512], F32, name="sp")
+                nc.tensor.matmul_mx(
+                    out=sp[:],
+                    lhsT=qq[:, i, :].bitcast(FP8X4), lhsT_scale=qs[:, i, :],
+                    rhs=kq[:, 2 * b + c, :].bitcast(FP8X4), rhs_scale=ks[:, 2 * b + c, :],
+                    start=True, stop=True,
+                )
+                live[("sp", i, c)] = sp
+
+        def rmax(i):
+            nm = small.tile([P, 2], F32, name="nm")
+            for c in range(2):
+                nc.vector.tensor_reduce(
+                    out=nm[:, c:c + 1], in_=live[("sp", i, c)][:], axis=AX.X, op=ALU.max, negate=True,
+                )
+            nmx = small.tile([P, 1], F32, name="nmx")
+            nc.vector.tensor_tensor(out=nmx[:], in0=nm[:, 0:1], in1=nm[:, 1:2], op=ALU.min)
+            live[("nmx", i)] = nmx
+
+        def expo(i):
+            nmx = live.pop(("nmx", i))
+            ee = stage.tile([P, 1024], F32, name="ee")
+            sm = small.tile([P, 2], F32, name="sm")
+            for c in range(2):
+                sp = live.pop(("sp", i, c))
+                nc.scalar.activation(
+                    out=ee[:, c * 512:(c + 1) * 512], in_=sp[:], func=ACT.Exp,
+                    bias=nmx[:, 0:1], scale=1.0, accum_out=sm[:, c:c + 1],
+                )
+            live[("ee", i)] = ee
+            live[("sm", i)] = sm
+
+        def fin(i):
+            ee = live.pop(("ee", i))
+            sm = live.pop(("sm", i))
+            tot = small.tile([P, 1], F32, name="tot")
+            nc.vector.tensor_tensor(out=tot[:], in0=sm[:, 0:1], in1=sm[:, 1:2], op=ALU.add)
+            rs = small.tile([P, 1], F32, name="rs")
+            nc.vector.reciprocal(out=rs[:], in_=tot[:])
+            oo = stage.tile([P, 1024], F32, name="oo")
+            nc.vector.scalar_tensor_tensor(
+                out=oo[:], in0=ee[:], scalar=rs[:, 0:1], in1=mraw[:, i * 1024:(i + 1) * 1024],
+                op0=ALU.mult, op1=ALU.mult,
+            )
+            nc.sync.dma_start(
+                out=out[i // 2].rearrange("(r a) m -> r a m", a=2)[:, i % 2, :], in_=oo[:],
+            )
+
+        wreg(0, 0, "v")
+        wreg(0, 1, "s")
+        wreg(1, 0, "v")
+        wreg(1, 1, "s")
+        t_x(0)
+        t_x(1)
+        qz_w(0)
+        qz_w(1)
+        e_x(0)
+        e_x(1)
+        t_k(0)
+        qz_x(0)
+        m1(0)
+        qz_x(1)
+        e_k(0)
+        t_k(1)
+        m1(1)
+        badd(0)
+        qz_k(0)
+        e_k(1)
+        badd(1)
+        qz_q(0)
+        qz_q(1)
+        qz_k(1)
+        m2(0)
+        t_x(2)
+        t_k(2)
+        e_k(2)
+        m2(1)
+
+        for i in range(4):
+            e_x(i + 2)
+            t_x(i + 3)
+            t_k(i + 3)
+            rmax(i)
+            expo(i)
+            e_k(i + 3)
+            qz_x(i + 2)
+            m1(i + 2)
+            qz_k(i + 2)
+            badd(i + 2)
+            if i > 0:
+                m2(i + 1)
+            fin(i)
+            qz_q(i + 2)
+        m2(5)
+        rmax(4)
+        expo(4)
+        rmax(5)
+        expo(5)
+        fin(4)
+        fin(5)

@@ -18,6 +18,7 @@ NT = 6
 FLOPS = 2 * B * N * TC * DQK + 2 * B * N * M * DQK
 
 PIN = False
+MODES = "GGGGVV"
 
 
 def tile_text2imgca_pa_kernel(tc, x1, Wq, bq, k_img, masks, out):
@@ -256,7 +257,7 @@ def tile_text2imgca_pa_kernel(tc, x1, Wq, bq, k_img, masks, out):
 
         def expo(i):
             nmx = live.pop(("nmx", i))
-            ee = stage.tile([P, 1024], F32, name="ee")
+            ee = stage.tile([P, 1024], F32, name="ee", bufs=4)
             sm = small.tile([P, 2], F32, name="sm")
             for c in range(2):
                 sp = live.pop(("sp", i, c))
@@ -267,21 +268,58 @@ def tile_text2imgca_pa_kernel(tc, x1, Wq, bq, k_img, masks, out):
             live[("ee", i)] = ee
             live[("sm", i)] = sm
 
-        def fin(i):
-            ee = live.pop(("ee", i))
+        def norm(i):
             sm = live.pop(("sm", i))
             tot = small.tile([P, 1], F32, name="tot")
             nc.vector.tensor_tensor(out=tot[:], in0=sm[:, 0:1], in1=sm[:, 1:2], op=ALU.add)
             rs = small.tile([P, 1], F32, name="rs")
             nc.vector.reciprocal(out=rs[:], in_=tot[:])
+            live[("rs", i)] = rs
+
+        def store(i, t):
+            nc.sync.dma_start(
+                out=out[i // 2].rearrange("(r a) m -> r a m", a=2)[:, i % 2, :], in_=t[:],
+            )
+
+        def fin(i):
+            ee = live.pop(("ee", i))
+            rs = live.pop(("rs", i))
             oo = stage.tile([P, 1024], F32, name="oo")
             nc.vector.scalar_tensor_tensor(
                 out=oo[:], in0=ee[:], scalar=rs[:, 0:1], in1=mraw[:, i * 1024:(i + 1) * 1024],
                 op0=ALU.mult, op1=ALU.mult,
             )
-            nc.sync.dma_start(
-                out=out[i // 2].rearrange("(r a) m -> r a m", a=2)[:, i % 2, :], in_=oo[:],
-            )
+            store(i, oo)
+
+        def gmul(i):
+            ee = live[("ee", i)]
+            for c in range(2):
+                nc.gpsimd.tensor_tensor(
+                    out=ee[:, c * 512:(c + 1) * 512], in0=ee[:, c * 512:(c + 1) * 512],
+                    in1=mraw[:, i * 1024 + c * 512: i * 1024 + (c + 1) * 512], op=ALU.mult,
+                )
+
+        def scale(i, eng):
+            ee = live.pop(("ee", i))
+            rs = live.pop(("rs", i))
+            if eng == "G":
+                nc.gpsimd.tensor_scalar(
+                    out=ee[:], in0=ee[:], scalar1=rs[:, 0:1], scalar2=0.0, op0=ALU.mult, op1=ALU.add,
+                )
+            elif eng == "S":
+                nc.scalar.activation(out=ee[:], in_=ee[:], func=ACT.Copy, scale=rs[:, 0:1])
+            else:
+                nc.vector.tensor_scalar(
+                    out=ee[:], in0=ee[:], scalar1=rs[:, 0:1], scalar2=None, op0=ALU.mult,
+                )
+            store(i, ee)
+
+        def tailf(i):
+            norm(i)
+            if MODES[i] == "V":
+                fin(i)
+            else:
+                scale(i, MODES[i])
 
         wreg(0, 0, "v")
         wreg(0, 1, "s")
@@ -302,36 +340,43 @@ def tile_text2imgca_pa_kernel(tc, x1, Wq, bq, k_img, masks, out):
         m1(1)
         badd(0)
         qz_k(0)
-        e_k(1)
+        e_k(1, ("s", "v"))
         badd(1)
         qz_q(0)
         qz_q(1)
         qz_k(1)
-        m2(0)
         t_x(2)
         t_k(2)
+        m2(0)
+        e_x(2)
         e_k(2)
         m2(1)
 
         for i in range(4):
-            e_x(i + 2)
             t_x(i + 3)
             t_k(i + 3)
             rmax(i)
             expo(i)
-            e_k(i + 3)
+            if MODES[i] != "V":
+                gmul(i)
             qz_x(i + 2)
             m1(i + 2)
             qz_k(i + 2)
+            e_x(i + 3)
+            e_k(i + 3)
             badd(i + 2)
             if i > 0:
                 m2(i + 1)
-            fin(i)
+            tailf(i)
             qz_q(i + 2)
         m2(5)
         rmax(4)
         expo(4)
+        if MODES[4] != "V":
+            gmul(4)
         rmax(5)
         expo(5)
-        fin(4)
-        fin(5)
+        if MODES[5] != "V":
+            gmul(5)
+        tailf(4)
+        tailf(5)

@@ -17,9 +17,6 @@ B, N, TC, DQK, M = 3, 256, 1024, 512, 1024
 NT = 6
 FLOPS = 2 * B * N * TC * DQK + 2 * B * N * M * DQK
 
-PIN = False
-MODES = "GGGGVV"
-
 
 def tile_text2imgca_pa_kernel(tc, x1, Wq, bq, k_img, masks, out):
     nc = tc.nc
@@ -27,8 +24,7 @@ def tile_text2imgca_pa_kernel(tc, x1, Wq, bq, k_img, masks, out):
         keep = ctx.enter_context(tc.tile_pool(name="keep", bufs=1))
         stage = ctx.enter_context(tc.tile_pool(name="stage", bufs=3))
         small = ctx.enter_context(tc.tile_pool(name="small", bufs=4))
-        tpool = ctx.enter_context(tc.psum_pool(name="tpool", bufs=3))
-        qpool = ctx.enter_context(tc.psum_pool(name="qpool", bufs=1))
+        tpool = ctx.enter_context(tc.psum_pool(name="tpool", bufs=4))
         spool = ctx.enter_context(tc.psum_pool(name="spool", bufs=4))
 
         ident = keep.tile([P, P], F32, name="ident")
@@ -51,8 +47,7 @@ def tile_text2imgca_pa_kernel(tc, x1, Wq, bq, k_img, masks, out):
         warm = keep.tile([P, 1], F32, name="warm")
         warm2 = keep.tile([P, 1], F32, name="warm2")
 
-        if PIN:
-            ctx.enter_context(tc.manual_schedule())
+        ctx.enter_context(tc.manual_schedule())
 
         with nc.allow_non_contiguous_dma(reason="bias: 256 pieces of 4 bytes, once"):
             nc.scalar.dma_start(
@@ -62,70 +57,53 @@ def tile_text2imgca_pa_kernel(tc, x1, Wq, bq, k_img, masks, out):
         nc.vector.memset(warm[:], 0.0)
         nc.scalar.activation(out=warm2[:], in_=warm[:], func=ACT.Exp)
 
-        def load_w(g):
+        def ld_w(g):
             nc.sync.dma_start(
                 out=wraw[:, g * 2048:(g + 1) * 2048].rearrange("p (u f) -> p u f", u=2),
                 in_=Wq[g * 512:(g + 1) * 512, :].rearrange("(u q e) c -> q u (e c)", u=2, q=P, e=2),
             )
 
-        def load_x(b):
+        def ld_x(b):
             nc.sync.dma_start(
                 out=xraw[:, b * 2048:(b + 1) * 2048],
                 in_=x1[b].rearrange("(r a) k -> r (a k)", a=2),
             )
 
-        def load_k(b, c):
+        def ld_k(i):
+            b, c = i // 2, i % 2
             nc.sync.dma_start(
-                out=kraw[:, b * 4096 + c * 2048: b * 4096 + (c + 1) * 2048].rearrange("p (c f) -> p c f", c=2),
+                out=kraw[:, i * 2048:(i + 1) * 2048].rearrange("p (c f) -> p c f", c=2),
                 in_=k_img[b, c * 512:(c + 1) * 512, :].rearrange("(c r a) d -> r c (a d)", c=2, r=P, a=2),
             )
 
-        def load_m(b):
+        def ld_m(b):
             nc.sync.dma_start(
                 out=mraw[:, b * 2048:(b + 1) * 2048],
                 in_=masks[b].rearrange("(r a) m -> r (a m)", a=2),
             )
 
-        load_w(0)
-        load_w(1)
-        load_x(0)
-        load_k(0, 0)
-        load_k(0, 1)
-        load_x(1)
-        load_k(1, 0)
-        load_k(1, 1)
-        load_m(0)
-        load_x(2)
-        load_k(2, 0)
-        load_k(2, 1)
-        load_m(1)
-        load_m(2)
-
         xw = xraw[:].bitcast(F32)
         kw = kraw[:].bitcast(F32)
-
         wgv = wg[:].rearrange("p (g u e m j) -> p g u e m j", g=2, u=2, e=2, m=P, j=4)
         wrv = wraw[:].rearrange("p (g j u m e) -> p g j u m e", g=2, j=4, u=2, m=P, e=2)
+        live = {}
 
-        def wreg(g, e, eng):
-            dst = wgv[:, g, :, e]
-            srcv = wrv[:, g, :, :, :, e].rearrange("p j u m -> p u m j")
-            if eng == "v":
+        def copy_out(eng, dst, srcv):
+            if eng == "V":
                 nc.vector.tensor_copy(out=dst, in_=srcv)
             else:
                 nc.scalar.copy(out=dst, in_=srcv)
 
-        def qz_w(g):
+        def wreg(g, e, eng):
+            copy_out(eng, wgv[:, g, :, e], wrv[:, g, :, :, :, e].rearrange("p j u m -> p u m j"))
+
+        def qzw(g):
             nc.vector.quantize_mx(
                 out=wq[:, g, :].bitcast(FP8X4), scales=ws[:, g, :],
                 in_=wg[:, g * 2048:(g + 1) * 2048],
             )
 
-        live = {}
-
-        def t_x(i):
-            if i >= NT:
-                return
+        def tx(i):
             tp = tpool.tile([P, 512], F32, name="tp")
             for s in range(4):
                 nc.tensor.transpose(
@@ -135,15 +113,7 @@ def tile_text2imgca_pa_kernel(tc, x1, Wq, bq, k_img, masks, out):
                 )
             live[("tx", i)] = tp
 
-        def copy_out(eng, dst, srcv):
-            if eng == "v":
-                nc.vector.tensor_copy(out=dst, in_=srcv)
-            else:
-                nc.scalar.copy(out=dst, in_=srcv)
-
-        def e_x(i, eng="s"):
-            if i >= NT:
-                return
+        def ex(i, eng):
             tp = live.pop(("tx", i))
             xg = stage.tile([P, 512], F32, name="xg", align_bytes=64)
             copy_out(
@@ -153,51 +123,41 @@ def tile_text2imgca_pa_kernel(tc, x1, Wq, bq, k_img, masks, out):
             )
             live[("xg", i)] = xg
 
-        def qz_x(i):
-            if i >= NT:
-                return
+        def qzx(i):
             xg = live.pop(("xg", i))
             nc.vector.quantize_mx(
                 out=xq[:, i, :].bitcast(FP8X4), scales=xs[:, i, :], in_=xg[:].bitcast(BF16),
             )
 
-        def t_k(i):
-            if i >= NT:
-                return
-            for h in range(2):
-                tp = tpool.tile([P, 512], F32, name="tp")
-                for s in range(4):
-                    base = i * 1024 + h * 512 + s * P
-                    nc.tensor.transpose(
-                        out=tp[:, s * P:(s + 1) * P], in_=kw[:, base: base + P], identity=ident[:],
-                    )
-                live[("tk", i, h)] = tp
-
-        def e_k(i, engs=("s", "s")):
-            if i >= NT:
-                return
-            kg = stage.tile([P, 1024], F32, name="kg", align_bytes=64)
-            for h in range(2):
-                tp = live.pop(("tk", i, h))
-                copy_out(
-                    engs[h],
-                    kg[:, h * 512:(h + 1) * 512].rearrange("p (r s) -> p r s", s=4),
-                    tp[:].rearrange("p (s r) -> p r s", s=4),
+        def tk(i, h):
+            tp = tpool.tile([P, 512], F32, name="tp")
+            for s in range(4):
+                base = i * 1024 + h * 512 + s * P
+                nc.tensor.transpose(
+                    out=tp[:, s * P:(s + 1) * P], in_=kw[:, base: base + P], identity=ident[:],
                 )
-            live[("kg", i)] = kg
+            live[("tk", i, h)] = tp
 
-        def qz_k(i):
-            if i >= NT:
-                return
+        def ek(i, h, eng):
+            if ("kg", i) not in live:
+                kg_new = stage.tile([P, 1024], F32, name="kg", align_bytes=64)
+                live[("kg", i)] = kg_new
+            kg = live[("kg", i)]
+            tp = live.pop(("tk", i, h))
+            copy_out(
+                eng,
+                kg[:, h * 512:(h + 1) * 512].rearrange("p (r s) -> p r s", s=4),
+                tp[:].rearrange("p (s r) -> p r s", s=4),
+            )
+
+        def qzk(i):
             kg = live.pop(("kg", i))
             nc.vector.quantize_mx(
                 out=kq[:, i, :].bitcast(FP8X4), scales=ks[:, i, :], in_=kg[:].bitcast(BF16),
             )
 
         def m1(i):
-            if i >= NT:
-                return
-            qp = qpool.tile([P, 512], F32, name="qp")
+            qp = tpool.tile([P, 512], F32, name="tp")
             for t in range(4):
                 for g in range(2):
                     nc.tensor.matmul_mx(
@@ -211,8 +171,6 @@ def tile_text2imgca_pa_kernel(tc, x1, Wq, bq, k_img, masks, out):
             live[("qp", i)] = qp
 
         def badd(i):
-            if i >= NT:
-                return
             qp = live.pop(("qp", i))
             qg = stage.tile([P, 512], BF16, name="qg", align_bytes=64)
             nc.vector.tensor_tensor(
@@ -223,160 +181,228 @@ def tile_text2imgca_pa_kernel(tc, x1, Wq, bq, k_img, masks, out):
             )
             live[("qg", i)] = qg
 
-        def qz_q(i):
-            if i >= NT:
-                return
+        def qzq(i):
             qg = live.pop(("qg", i))
             nc.vector.quantize_mx(
                 out=qq[:, i, :].bitcast(FP8X4), scales=qs[:, i, :], in_=qg[:],
             )
 
-        def m2(i):
-            if i >= NT:
-                return
+        def m2(i, c):
             b = i // 2
-            for c in range(2):
-                sp = spool.tile([P, 512], F32, name="sp")
-                nc.tensor.matmul_mx(
-                    out=sp[:],
-                    lhsT=qq[:, i, :].bitcast(FP8X4), lhsT_scale=qs[:, i, :],
-                    rhs=kq[:, 2 * b + c, :].bitcast(FP8X4), rhs_scale=ks[:, 2 * b + c, :],
-                    start=True, stop=True,
-                )
-                live[("sp", i, c)] = sp
+            sp = spool.tile([P, 512], F32, name="sp")
+            nc.tensor.matmul_mx(
+                out=sp[:],
+                lhsT=qq[:, i, :].bitcast(FP8X4), lhsT_scale=qs[:, i, :],
+                rhs=kq[:, 2 * b + c, :].bitcast(FP8X4), rhs_scale=ks[:, 2 * b + c, :],
+                start=True, stop=True,
+            )
+            live[("sp", i, c)] = sp
 
-        def rmax(i):
-            nm = small.tile([P, 2], F32, name="nm")
-            for c in range(2):
-                nc.vector.tensor_reduce(
-                    out=nm[:, c:c + 1], in_=live[("sp", i, c)][:], axis=AX.X, op=ALU.max, negate=True,
-                )
-            nmx = small.tile([P, 1], F32, name="nmx")
-            nc.vector.tensor_tensor(out=nmx[:], in0=nm[:, 0:1], in1=nm[:, 1:2], op=ALU.min)
-            live[("nmx", i)] = nmx
-
-        def expo(i):
-            nmx = live.pop(("nmx", i))
-            ee = stage.tile([P, 1024], F32, name="ee", bufs=4)
-            sm = small.tile([P, 2], F32, name="sm")
-            for c in range(2):
-                sp = live.pop(("sp", i, c))
-                nc.scalar.activation(
-                    out=ee[:, c * 512:(c + 1) * 512], in_=sp[:], func=ACT.Exp,
-                    bias=nmx[:, 0:1], scale=1.0, accum_out=sm[:, c:c + 1],
-                )
-            live[("ee", i)] = ee
-            live[("sm", i)] = sm
-
-        def norm(i):
-            sm = live.pop(("sm", i))
-            tot = small.tile([P, 1], F32, name="tot")
-            nc.vector.tensor_tensor(out=tot[:], in0=sm[:, 0:1], in1=sm[:, 1:2], op=ALU.add)
-            rs = small.tile([P, 1], F32, name="rs")
-            nc.vector.reciprocal(out=rs[:], in_=tot[:])
-            live[("rs", i)] = rs
-
-        def store(i, t):
-            nc.sync.dma_start(
-                out=out[i // 2].rearrange("(r a) m -> r a m", a=2)[:, i % 2, :], in_=t[:],
+        def mx(i, c):
+            if c == 0:
+                nm_new = small.tile([P, 2], F32, name="nm")
+                live[("nm", i)] = nm_new
+            nm = live[("nm", i)]
+            nc.vector.tensor_reduce(
+                out=nm[:, c:c + 1], in_=live[("sp", i, c)][:], axis=AX.X, op=ALU.max, negate=True,
             )
 
-        def fin(i):
-            ee = live.pop(("ee", i))
-            rs = live.pop(("rs", i))
-            oo = stage.tile([P, 1024], F32, name="oo")
-            nc.vector.scalar_tensor_tensor(
-                out=oo[:], in0=ee[:], scalar=rs[:, 0:1], in1=mraw[:, i * 1024:(i + 1) * 1024],
-                op0=ALU.mult, op1=ALU.mult,
-            )
-            store(i, oo)
+        def nmx(i):
+            nm = live.pop(("nm", i))
+            nmn = small.tile([P, 1], F32, name="nmn")
+            nc.vector.tensor_tensor(out=nmn[:], in0=nm[:, 0:1], in1=nm[:, 1:2], op=ALU.min)
+            live[("nmn", i)] = nmn
 
-        def gmul(i):
+        def expo(i, c):
+            if c == 0:
+                ee_new = stage.tile([P, 1024], F32, name="ee", bufs=4)
+                sm_new = small.tile([P, 2], F32, name="sm")
+                live[("ee", i)] = ee_new
+                live[("sm", i)] = sm_new
             ee = live[("ee", i)]
-            for c in range(2):
-                nc.gpsimd.tensor_tensor(
-                    out=ee[:, c * 512:(c + 1) * 512], in0=ee[:, c * 512:(c + 1) * 512],
-                    in1=mraw[:, i * 1024 + c * 512: i * 1024 + (c + 1) * 512], op=ALU.mult,
-                )
+            sm = live[("sm", i)]
+            sp = live.pop(("sp", i, c))
+            nc.scalar.activation(
+                out=ee[:, c * 512:(c + 1) * 512], in_=sp[:], func=ACT.Exp,
+                bias=live[("nmn", i)][:, 0:1], scale=1.0, accum_out=sm[:, c:c + 1],
+            )
 
-        def scale(i, eng):
-            ee = live.pop(("ee", i))
-            rs = live.pop(("rs", i))
-            if eng == "G":
-                nc.gpsimd.tensor_scalar(
-                    out=ee[:], in0=ee[:], scalar1=rs[:, 0:1], scalar2=0.0, op0=ALU.mult, op1=ALU.add,
-                )
-            elif eng == "S":
-                nc.scalar.activation(out=ee[:], in_=ee[:], func=ACT.Copy, scale=rs[:, 0:1])
-            else:
-                nc.vector.tensor_scalar(
-                    out=ee[:], in0=ee[:], scalar1=rs[:, 0:1], scalar2=None, op0=ALU.mult,
-                )
-            store(i, ee)
+        def tot(i):
+            sm = live.pop(("sm", i))
+            tt = small.tile([P, 1], F32, name="tt")
+            nc.vector.tensor_tensor(out=tt[:], in0=sm[:, 0:1], in1=sm[:, 1:2], op=ALU.add)
+            live[("tt", i)] = tt
 
-        def tailf(i):
-            norm(i)
-            if MODES[i] == "V":
-                fin(i)
-            else:
-                scale(i, MODES[i])
+        def rs(i):
+            tt = live.pop(("tt", i))
+            rr = small.tile([P, 1], F32, name="rr")
+            nc.vector.reciprocal(out=rr[:], in_=tt[:])
+            live[("rr", i)] = rr
 
-        wreg(0, 0, "v")
-        wreg(0, 1, "s")
-        wreg(1, 0, "v")
-        wreg(1, 1, "s")
-        t_x(0)
-        t_x(1)
-        qz_w(0)
-        qz_w(1)
-        e_x(0)
-        e_x(1)
-        t_k(0)
-        qz_x(0)
+        def fin(i, lo=0, hi=1024):
+            if lo == 0:
+                oo_new = stage.tile([P, 1024], F32, name="oo")
+                live[("oo", i)] = oo_new
+            nc.vector.scalar_tensor_tensor(
+                out=live[("oo", i)][:, lo:hi], in0=live[("ee", i)][:, lo:hi], scalar=live[("rr", i)][:, 0:1],
+                in1=mraw[:, i * 1024 + lo: i * 1024 + hi], op0=ALU.mult, op1=ALU.mult,
+            )
+
+        def st(i, lo=0, hi=1024):
+            nc.sync.dma_start(
+                out=out[i // 2].rearrange("(r a) m -> r a m", a=2)[:, i % 2, lo:hi],
+                in_=live[("oo", i)][:, lo:hi],
+            )
+
+        ld_w(0)
+        ld_w(1)
+        ld_x(0)
+        ld_x(1)
+        ld_k(0)
+        ld_k(1)
+        ld_x(2)
+        ld_m(0)
+        ld_k(2)
+        ld_k(3)
+        ld_m(1)
+        ld_k(4)
+        ld_k(5)
+        ld_m(2)
+        wreg(0, 0, "V")
+        wreg(0, 1, "S")
+        wreg(1, 0, "V")
+        wreg(1, 1, "S")
+        qzw(0)
+        tx(0)
+        tx(1)
+        qzw(1)
+        ex(0, "S")
+        ex(1, "S")
+        tx(2)
+        qzx(0)
+        tx(3)
+        ex(2, "S")
+        qzx(1)
         m1(0)
-        qz_x(1)
-        e_k(0)
-        t_k(1)
-        m1(1)
+        ex(3, "S")
+        qzx(2)
+        tk(0, 0)
         badd(0)
-        qz_k(0)
-        e_k(1, ("s", "v"))
+        tk(0, 1)
+        ek(0, 0, "S")
+        m1(1)
+        qzx(3)
+        ek(0, 1, "S")
+        tk(1, 0)
         badd(1)
-        qz_q(0)
-        qz_q(1)
-        qz_k(1)
-        t_x(2)
-        t_k(2)
-        m2(0)
-        e_x(2)
-        e_k(2)
-        m2(1)
-
-        for i in range(4):
-            t_x(i + 3)
-            t_k(i + 3)
-            rmax(i)
-            expo(i)
-            if MODES[i] != "V":
-                gmul(i)
-            qz_x(i + 2)
-            m1(i + 2)
-            qz_k(i + 2)
-            e_x(i + 3)
-            e_k(i + 3)
-            badd(i + 2)
-            if i > 0:
-                m2(i + 1)
-            tailf(i)
-            qz_q(i + 2)
-        m2(5)
-        rmax(4)
-        expo(4)
-        if MODES[4] != "V":
-            gmul(4)
-        rmax(5)
-        expo(5)
-        if MODES[5] != "V":
-            gmul(5)
-        tailf(4)
-        tailf(5)
+        tk(1, 1)
+        ek(1, 0, "S")
+        m1(2)
+        qzq(0)
+        qzk(0)
+        ek(1, 1, "S")
+        m1(3)
+        badd(2)
+        tx(4)
+        qzq(1)
+        qzk(1)
+        tk(2, 0)
+        ex(4, "S")
+        tk(2, 1)
+        badd(3)
+        m2(0, 0)
+        ek(2, 0, "S")
+        m2(0, 1)
+        qzq(2)
+        qzq(3)
+        m2(1, 0)
+        ek(2, 1, "S")
+        mx(0, 0)
+        m2(1, 1)
+        tx(5)
+        mx(0, 1)
+        tk(3, 0)
+        nmx(0)
+        qzx(4)
+        tk(3, 1)
+        expo(0, 0)
+        qzk(2)
+        m1(4)
+        expo(0, 1)
+        mx(1, 0)
+        mx(1, 1)
+        ex(5, "S")
+        nmx(1)
+        ek(3, 0, "S")
+        tot(0)
+        tk(4, 0)
+        rs(0)
+        fin(0)
+        ek(3, 1, "S")
+        tk(4, 1)
+        m2(2, 0)
+        expo(1, 0)
+        qzx(5)
+        st(0)
+        qzk(3)
+        expo(1, 1)
+        badd(4)
+        ek(4, 0, "S")
+        m2(2, 1)
+        m1(5)
+        mx(2, 0)
+        ek(4, 1, "S")
+        mx(2, 1)
+        m2(3, 0)
+        m2(3, 1)
+        nmx(2)
+        tk(5, 0)
+        tot(1)
+        rs(1)
+        expo(2, 0)
+        fin(1)
+        tk(5, 1)
+        expo(2, 1)
+        qzq(4)
+        ek(5, 0, "S")
+        st(1)
+        badd(5)
+        ek(5, 1, "S")
+        qzk(4)
+        mx(3, 0)
+        m2(4, 0)
+        mx(3, 1)
+        nmx(3)
+        tot(2)
+        rs(2)
+        expo(3, 0)
+        fin(2)
+        expo(3, 1)
+        qzq(5)
+        st(2)
+        qzk(5)
+        mx(4, 0)
+        m2(4, 1)
+        m2(5, 0)
+        mx(4, 1)
+        m2(5, 1)
+        nmx(4)
+        tot(3)
+        rs(3)
+        expo(4, 0)
+        fin(3)
+        expo(4, 1)
+        mx(5, 0)
+        st(3)
+        mx(5, 1)
+        nmx(5)
+        tot(4)
+        rs(4)
+        expo(5, 0)
+        fin(4)
+        expo(5, 1)
+        st(4)
+        tot(5)
+        rs(5)
+        fin(5)
+        st(5)

@@ -47,13 +47,8 @@ def tile_text2imgca_pa_kernel(tc, x1, Wq, bq, k_img, masks, out):
         warm = keep.tile([P, 1], F32, name="warm")
         warm2 = keep.tile([P, 1], F32, name="warm2")
 
-        ctx.enter_context(tc.manual_schedule())
+        pass
 
-        with nc.allow_non_contiguous_dma(reason="bias: 256 pieces of 4 bytes, once"):
-            nc.scalar.dma_start(
-                out=bias[:].rearrange("p (u e) -> p u e", u=2),
-                in_=bq.rearrange("(u p e) -> p u e", u=2, p=P, e=2),
-            )
         nc.vector.memset(warm[:], 0.0)
         nc.scalar.activation(out=warm2[:], in_=warm[:], func=ACT.Exp)
 
@@ -72,8 +67,8 @@ def tile_text2imgca_pa_kernel(tc, x1, Wq, bq, k_img, masks, out):
         def ld_k(i):
             b, c = i // 2, i % 2
             nc.sync.dma_start(
-                out=kraw[:, i * 2048:(i + 1) * 2048].rearrange("p (c f) -> p c f", c=2),
-                in_=k_img[b, c * 512:(c + 1) * 512, :].rearrange("(c r a) d -> r c (a d)", c=2, r=P, a=2),
+                out=kraw[:, i * 2048:(i + 1) * 2048],
+                in_=k_img[b, c * 512:(c + 1) * 512, :].rearrange("(r a) d -> r (a d)", a=4),
             )
 
         def ld_m(b):
@@ -146,7 +141,7 @@ def tile_text2imgca_pa_kernel(tc, x1, Wq, bq, k_img, masks, out):
             tp = live.pop(("tk", i, h))
             copy_out(
                 eng,
-                kg[:, h * 512:(h + 1) * 512].rearrange("p (r s) -> p r s", s=4),
+                kg[:].rearrange("p (r h s) -> p h r s", h=2, s=4)[:, h],
                 tp[:].rearrange("p (s r) -> p r s", s=4),
             )
 
@@ -199,7 +194,7 @@ def tile_text2imgca_pa_kernel(tc, x1, Wq, bq, k_img, masks, out):
             live[("sp", i, c)] = sp
 
         def mx(i, c):
-            if c == 0:
+            if ("nm", i) not in live:
                 nm_new = small.tile([P, 2], F32, name="nm")
                 live[("nm", i)] = nm_new
             nm = live[("nm", i)]
@@ -230,7 +225,7 @@ def tile_text2imgca_pa_kernel(tc, x1, Wq, bq, k_img, masks, out):
         def tot(i):
             sm = live.pop(("sm", i))
             tt = small.tile([P, 1], F32, name="tt")
-            nc.vector.tensor_tensor(out=tt[:], in0=sm[:, 0:1], in1=sm[:, 1:2], op=ALU.add)
+            nc.scalar.activation(out=tt[:], in_=sm[:, 0:1], func=ACT.Identity, bias=sm[:, 1:2], scale=1.0)
             live[("tt", i)] = tt
 
         def rs(i):
@@ -257,6 +252,11 @@ def tile_text2imgca_pa_kernel(tc, x1, Wq, bq, k_img, masks, out):
         ld_w(0)
         ld_w(1)
         ld_x(0)
+        with nc.allow_non_contiguous_dma(reason="bias: 256 pieces of 4 bytes, once"):
+            nc.sync.dma_start(
+                out=bias[:].rearrange("p (u e) -> p u e", u=2),
+                in_=bq.rearrange("(u p e) -> p u e", u=2, p=P, e=2),
+            )
         ld_x(1)
         ld_k(0)
         ld_k(1)
@@ -404,5 +404,7 @@ def tile_text2imgca_pa_kernel(tc, x1, Wq, bq, k_img, masks, out):
         st(4)
         tot(5)
         rs(5)
-        fin(5)
-        st(5)
+        fin(5, 0, 512)
+        st(5, 0, 512)
+        fin(5, 512, 1024)
+        st(5, 512, 1024)

@@ -258,9 +258,9 @@ def tile_text2imgca_pa_kernel(tc, x1, Wq, bq, k_img, masks, out):
                 in_=bq.rearrange("(u p e) -> p u e", u=2, p=P, e=2),
             )
         ld_x(1)
+        ld_x(2)
         ld_k(0)
         ld_k(1)
-        ld_x(2)
         ld_m(0)
         ld_k(2)
         ld_k(3)
@@ -286,90 +286,91 @@ def tile_text2imgca_pa_kernel(tc, x1, Wq, bq, k_img, masks, out):
         m1(0)
         ex(3, "S")
         qzx(2)
-        tk(0, 0)
+        tx(4)
         badd(0)
-        tk(0, 1)
-        ek(0, 0, "S")
+        tx(5)
+        ex(4, "S")
         m1(1)
         qzx(3)
-        ek(0, 1, "S")
-        tk(1, 0)
+        ex(5, "S")
+        m1(2)
         badd(1)
+        tk(0, 0)
+        qzq(0)
+        qzx(4)
+        tk(0, 1)
+        ek(0, 0, "S")
+        badd(2)
+        m1(3)
+        ek(0, 1, "S")
+        qzq(1)
+        qzx(5)
+        tk(1, 0)
+        badd(3)
         tk(1, 1)
         ek(1, 0, "S")
-        m1(2)
-        qzq(0)
+        m1(4)
+        qzq(2)
         qzk(0)
         ek(1, 1, "S")
-        m1(3)
-        badd(2)
-        tx(4)
-        qzq(1)
-        qzk(1)
+        m1(5)
+        badd(4)
         tk(2, 0)
-        ex(4, "S")
-        tk(2, 1)
-        badd(3)
-        m2(0, 0)
-        ek(2, 0, "S")
-        m2(0, 1)
-        qzq(2)
         qzq(3)
-        m2(1, 0)
+        qzk(1)
+        tk(2, 1)
+        ek(2, 0, "S")
+        m2(0, 0)
+        badd(5)
         ek(2, 1, "S")
-        mx(0, 0)
+        m2(0, 1)
+        m2(1, 0)
+        qzq(4)
+        qzq(5)
         m2(1, 1)
-        tx(5)
-        mx(0, 1)
+        mx(0, 0)
         tk(3, 0)
-        nmx(0)
-        qzx(4)
+        mx(0, 1)
         tk(3, 1)
-        expo(0, 0)
-        qzk(2)
-        m1(4)
-        expo(0, 1)
-        mx(1, 0)
-        mx(1, 1)
-        ex(5, "S")
-        nmx(1)
-        ek(3, 0, "S")
-        tot(0)
         tk(4, 0)
+        nmx(0)
+        qzk(2)
+        tk(4, 1)
+        expo(0, 0)
+        mx(1, 0)
+        expo(0, 1)
+        m2(2, 0)
+        mx(1, 1)
+        ek(3, 0, "S")
+        nmx(1)
+        tot(0)
         rs(0)
         fin(0)
         ek(3, 1, "S")
-        tk(4, 1)
-        m2(2, 0)
         expo(1, 0)
-        qzx(5)
-        st(0)
         qzk(3)
         expo(1, 1)
-        badd(4)
+        st(0)
+        mx(2, 0)
         ek(4, 0, "S")
         m2(2, 1)
-        m1(5)
-        mx(2, 0)
-        ek(4, 1, "S")
-        mx(2, 1)
         m2(3, 0)
+        mx(2, 1)
+        ek(4, 1, "S")
         m2(3, 1)
-        nmx(2)
         tk(5, 0)
+        nmx(2)
         tot(1)
         rs(1)
         expo(2, 0)
-        fin(1)
         tk(5, 1)
+        fin(1)
         expo(2, 1)
-        qzq(4)
+        qzk(4)
         ek(5, 0, "S")
         st(1)
-        badd(5)
-        ek(5, 1, "S")
-        qzk(4)
         mx(3, 0)
+        ek(5, 1, "S")
         m2(4, 0)
         mx(3, 1)
         nmx(3)
@@ -378,9 +379,8 @@ def tile_text2imgca_pa_kernel(tc, x1, Wq, bq, k_img, masks, out):
         expo(3, 0)
         fin(2)
         expo(3, 1)
-        qzq(5)
-        st(2)
         qzk(5)
+        st(2)
         mx(4, 0)
         m2(4, 1)
         m2(5, 0)

@@ -268,6 +268,9 @@ def tile_text2imgca_pa_kernel(tc, x1, Wq, bq, k_img, masks, out):
         ld_k(4)
         ld_k(5)
         ld_m(2)
+        dummy = tpool.tile([P, 512], F32, name="tp")
+        for rep in range(4):
+            nc.tensor.matmul(out=dummy[:], lhsT=wraw[:, 0:P], rhs=wraw[:, 0:512], start=True, stop=True)
         wreg(0, 0, "V")
         wreg(0, 1, "S")
         wreg(1, 0, "V")

@@ -261,12 +261,12 @@ def tile_text2imgca_pa_kernel(tc, x1, Wq, bq, k_img, masks, out):
         ld_x(2)
         ld_k(0)
         ld_k(1)
-        ld_m(0)
         ld_k(2)
         ld_k(3)
-        ld_m(1)
         ld_k(4)
         ld_k(5)
+        ld_m(0)
+        ld_m(1)
         ld_m(2)
         dummy = tpool.tile([P, 512], F32, name="tp")
         for rep in range(4):

@@ -24,8 +24,7 @@ def tile_text2imgca_pa_kernel(tc, x1, Wq, bq, k_img, masks, out):
         keep = ctx.enter_context(tc.tile_pool(name="keep", bufs=1))
         stage = ctx.enter_context(tc.tile_pool(name="stage", bufs=3))
         small = ctx.enter_context(tc.tile_pool(name="small", bufs=4))
-        tpool = ctx.enter_context(tc.psum_pool(name="tpool", bufs=4))
-        spool = ctx.enter_context(tc.psum_pool(name="spool", bufs=4))
+        tpool = ctx.enter_context(tc.psum_pool(name="tpool", bufs=8))
 
         ident = keep.tile([P, P], F32, name="ident")
         make_identity(nc, ident[:])
@@ -184,7 +183,7 @@ def tile_text2imgca_pa_kernel(tc, x1, Wq, bq, k_img, masks, out):
 
         def m2(i, c):
             b = i // 2
-            sp = spool.tile([P, 512], F32, name="sp")
+            sp = tpool.tile([P, 512], F32, name="tp")
             nc.tensor.matmul_mx(
                 out=sp[:],
                 lhsT=qq[:, i, :].bitcast(FP8X4), lhsT_scale=qs[:, i, :],
@@ -287,41 +286,41 @@ def tile_text2imgca_pa_kernel(tc, x1, Wq, bq, k_img, masks, out):
         ex(2, "S")
         qzx(1)
         m1(0)
+        m1(1)
         ex(3, "S")
         qzx(2)
         tx(4)
         badd(0)
         tx(5)
+        tk(0, 0)
+        tk(0, 1)
         ex(4, "S")
-        m1(1)
         qzx(3)
         ex(5, "S")
         m1(2)
+        m1(3)
         badd(1)
-        tk(0, 0)
         qzq(0)
         qzx(4)
-        tk(0, 1)
         ek(0, 0, "S")
         badd(2)
-        m1(3)
         ek(0, 1, "S")
         qzq(1)
         qzx(5)
         tk(1, 0)
-        badd(3)
         tk(1, 1)
+        tk(2, 0)
+        tk(2, 1)
+        badd(3)
         ek(1, 0, "S")
         m1(4)
+        m1(5)
         qzq(2)
         qzk(0)
         ek(1, 1, "S")
-        m1(5)
         badd(4)
-        tk(2, 0)
         qzq(3)
         qzk(1)
-        tk(2, 1)
         ek(2, 0, "S")
         m2(0, 0)
         badd(5)

@@ -13,9 +13,19 @@ ACT = mybir.ActivationFunctionType
 AX = mybir.AxisListType
 
 P = 128
-B, N, TC, DQK, M = 3, 256, 1024, 512, 1024
-NT = 6
-FLOPS = 2 * B * N * TC * DQK + 2 * B * N * M * DQK
+PACK = 4
+K_PASS = PACK * P
+BANK = 512
+BATCH, TOKENS, D_TEXT, D_QK, PIXELS = 3, 256, 1024, 512, 1024
+TILES_A_BATCH = TOKENS // P
+N_TILES = BATCH * TILES_A_BATCH
+HALVES_A_BATCH = PIXELS // BANK
+N_HALVES = BATCH * HALVES_A_BATCH
+W_PASSES = D_TEXT // K_PASS
+Q_BLOCKS = D_QK // P
+WARM_UP_MATMULS = 4
+X_TILES_AHEAD = 3
+FLOPS = 2 * BATCH * TOKENS * D_TEXT * D_QK + 2 * BATCH * TOKENS * PIXELS * D_QK
 
 
 def tile_text2imgca_pa_kernel(tc, x1, Wq, bq, k_img, masks, out):
@@ -24,389 +34,314 @@ def tile_text2imgca_pa_kernel(tc, x1, Wq, bq, k_img, masks, out):
         keep = ctx.enter_context(tc.tile_pool(name="keep", bufs=1))
         stage = ctx.enter_context(tc.tile_pool(name="stage", bufs=3))
         small = ctx.enter_context(tc.tile_pool(name="small", bufs=4))
-        tpool = ctx.enter_context(tc.psum_pool(name="tpool", bufs=8))
+        psum = ctx.enter_context(tc.psum_pool(name="psum", bufs=8))
 
-        ident = keep.tile([P, P], F32, name="ident")
-        make_identity(nc, ident[:])
+        identity = keep.tile([P, P], F32, name="identity")
+        make_identity(nc, identity[:])
 
-        wraw = keep.tile([P, 4096], BF16, name="wraw")
-        wg = keep.tile([P, 4096], BF16, name="wg", align_bytes=64)
-        wq = keep.tile([P, 2, 512], U32, name="wq", align_bytes=64)
-        ws = keep.tile([P, 2, 512], U8, name="ws", align_bytes=64)
-        xraw = keep.tile([P, B * 2048], BF16, name="xraw")
-        xq = keep.tile([P, NT, 256], U32, name="xq", align_bytes=64)
-        xs = keep.tile([P, NT, 256], U8, name="xs", align_bytes=64)
-        kraw = keep.tile([P, B * 4096], BF16, name="kraw")
-        kq = keep.tile([P, NT, 512], U32, name="kq", align_bytes=64)
-        ks = keep.tile([P, NT, 512], U8, name="ks", align_bytes=64)
-        qq = keep.tile([P, NT, 128], U32, name="qq", align_bytes=64)
-        qs = keep.tile([P, NT, 128], U8, name="qs", align_bytes=64)
-        mraw = keep.tile([P, B * 2048], BF16, name="mraw")
-        bias = keep.tile([P, 4], BF16, name="bias")
-        warm = keep.tile([P, 1], F32, name="warm")
-        warm2 = keep.tile([P, 1], F32, name="warm2")
+        w_raw = keep.tile([P, W_PASSES * PACK * D_QK], BF16, name="w_raw")
+        w_grouped = keep.tile([P, W_PASSES * PACK * D_QK], BF16, name="w_grouped", align_bytes=64)
+        w_codes = keep.tile([P, W_PASSES, D_QK], U32, name="w_codes", align_bytes=64)
+        w_scales = keep.tile([P, W_PASSES, D_QK], U8, name="w_scales", align_bytes=64)
+        x_raw = keep.tile([P, N_TILES * D_TEXT], BF16, name="x_raw")
+        x_codes = keep.tile([P, N_TILES, W_PASSES * P], U32, name="x_codes", align_bytes=64)
+        x_scales = keep.tile([P, N_TILES, W_PASSES * P], U8, name="x_scales", align_bytes=64)
+        k_raw = keep.tile([P, N_HALVES * PACK * D_QK], BF16, name="k_raw")
+        k_codes = keep.tile([P, N_HALVES, BANK], U32, name="k_codes", align_bytes=64)
+        k_scales = keep.tile([P, N_HALVES, BANK], U8, name="k_scales", align_bytes=64)
+        q_codes = keep.tile([P, N_TILES, P], U32, name="q_codes", align_bytes=64)
+        q_scales = keep.tile([P, N_TILES, P], U8, name="q_scales", align_bytes=64)
+        mask_raw = keep.tile([P, N_TILES * PIXELS], BF16, name="mask_raw")
+        bias = keep.tile([P, Q_BLOCKS], BF16, name="bias")
+        exp_in = keep.tile([P, 1], F32, name="exp_in")
+        exp_out = keep.tile([P, 1], F32, name="exp_out")
 
-        pass
+        nc.vector.memset(exp_in[:], 0.0)
+        nc.scalar.activation(out=exp_out[:], in_=exp_in[:], func=ACT.Exp)
 
-        nc.vector.memset(warm[:], 0.0)
-        nc.scalar.activation(out=warm2[:], in_=warm[:], func=ACT.Exp)
 
-        def ld_w(g):
+        def load_w(g):
             nc.sync.dma_start(
-                out=wraw[:, g * 2048:(g + 1) * 2048].rearrange("p (u f) -> p u f", u=2),
-                in_=Wq[g * 512:(g + 1) * 512, :].rearrange("(u q e) c -> q u (e c)", u=2, q=P, e=2),
+                out=w_raw[:, g * PACK * D_QK:(g + 1) * PACK * D_QK].rearrange("p (u f) -> p u f", u=2),
+                in_=Wq[g * K_PASS:(g + 1) * K_PASS, :].rearrange("(u p e) n -> p u (e n)", u=2, p=P, e=2),
             )
 
-        def ld_x(b):
+        def load_bias():
+            with nc.allow_non_contiguous_dma(reason="bias: 256 pieces of 4 bytes, once"):
+                nc.sync.dma_start(
+                    out=bias[:].rearrange("p (u e) -> p u e", u=2),
+                    in_=bq.rearrange("(u p e) -> p u e", u=2, p=P, e=2),
+                )
+
+        def load_x(b):
             nc.sync.dma_start(
-                out=xraw[:, b * 2048:(b + 1) * 2048],
-                in_=x1[b].rearrange("(r a) k -> r (a k)", a=2),
+                out=x_raw[:, b * TILES_A_BATCH * D_TEXT:(b + 1) * TILES_A_BATCH * D_TEXT],
+                in_=x1[b].rearrange("(r a) k -> r (a k)", a=TILES_A_BATCH),
             )
 
-        def ld_k(i):
-            b, c = i // 2, i % 2
+        def load_k(j):
+            first_pixel = (j % HALVES_A_BATCH) * BANK
             nc.sync.dma_start(
-                out=kraw[:, i * 2048:(i + 1) * 2048],
-                in_=k_img[b, c * 512:(c + 1) * 512, :].rearrange("(r a) d -> r (a d)", a=4),
+                out=k_raw[:, j * PACK * D_QK:(j + 1) * PACK * D_QK],
+                in_=k_img[j // HALVES_A_BATCH, first_pixel:first_pixel + BANK, :].rearrange("(r a) d -> r (a d)", a=4),
             )
 
-        def ld_m(b):
+        def load_mask(b):
             nc.sync.dma_start(
-                out=mraw[:, b * 2048:(b + 1) * 2048],
-                in_=masks[b].rearrange("(r a) m -> r (a m)", a=2),
+                out=mask_raw[:, b * TILES_A_BATCH * PIXELS:(b + 1) * TILES_A_BATCH * PIXELS],
+                in_=masks[b].rearrange("(r a) y -> r (a y)", a=TILES_A_BATCH),
             )
 
-        xw = xraw[:].bitcast(F32)
-        kw = kraw[:].bitcast(F32)
-        wgv = wg[:].rearrange("p (g u e m j) -> p g u e m j", g=2, u=2, e=2, m=P, j=4)
-        wrv = wraw[:].rearrange("p (g j u m e) -> p g j u m e", g=2, j=4, u=2, m=P, e=2)
-        live = {}
+        x_words = x_raw[:].bitcast(F32)
+        k_words = k_raw[:].bitcast(F32)
+        held = {}
 
-        def copy_out(eng, dst, srcv):
-            if eng == "V":
-                nc.vector.tensor_copy(out=dst, in_=srcv)
+
+        w_in = w_raw[:].rearrange("p (g t u m e) -> p g t u m e", g=W_PASSES, t=PACK, u=2, m=P, e=2)
+        w_out = w_grouped[:].rearrange("p (g u e m t) -> p g u e m t", g=W_PASSES, u=2, e=2, m=P, t=PACK)
+
+        def group_w(g, e, engine):
+            source = w_in[:, g, :, :, :, e].rearrange("p t u m -> p u m t")
+            if engine == "vector":
+                nc.vector.tensor_copy(out=w_out[:, g, :, e], in_=source)
             else:
-                nc.scalar.copy(out=dst, in_=srcv)
+                nc.scalar.copy(out=w_out[:, g, :, e], in_=source)
 
-        def wreg(g, e, eng):
-            copy_out(eng, wgv[:, g, :, e], wrv[:, g, :, :, :, e].rearrange("p j u m -> p u m j"))
-
-        def qzw(g):
+        def quantise_w(g):
             nc.vector.quantize_mx(
-                out=wq[:, g, :].bitcast(FP8X4), scales=ws[:, g, :],
-                in_=wg[:, g * 2048:(g + 1) * 2048],
+                out=w_codes[:, g, :].bitcast(FP8X4), scales=w_scales[:, g, :],
+                in_=w_grouped[:, g * PACK * D_QK:(g + 1) * PACK * D_QK],
             )
 
-        def tx(i):
-            tp = tpool.tile([P, 512], F32, name="tp")
-            for s in range(4):
+        def warm_up():
+            unread = psum.tile([P, BANK], F32, name="bank")
+            for repeat in range(WARM_UP_MATMULS):
+                nc.tensor.matmul(out=unread[:], lhsT=w_raw[:, 0:P], rhs=w_raw[:, 0:BANK], start=True, stop=True)
+
+
+        def transpose_words(words, first):
+            bank = psum.tile([P, BANK], F32, name="bank")
+            for s in range(BANK // P):
                 nc.tensor.transpose(
-                    out=tp[:, s * P:(s + 1) * P],
-                    in_=xw[:, i * 512 + s * P: i * 512 + (s + 1) * P],
-                    identity=ident[:],
+                    out=bank[:, s * P:(s + 1) * P], in_=words[:, first + s * P: first + (s + 1) * P],
+                    identity=identity[:],
                 )
-            live[("tx", i)] = tp
+            return bank
 
-        def ex(i, eng):
-            tp = live.pop(("tx", i))
-            xg = stage.tile([P, 512], F32, name="xg", align_bytes=64)
-            copy_out(
-                eng,
-                xg[:].rearrange("p (g r u) -> p g r u", g=2, r=P, u=2),
-                tp[:].rearrange("p (g u r) -> p g r u", g=2, u=2, r=P),
+        def transpose_x(i):
+            held[("x bank", i)] = transpose_words(x_words, i * BANK)
+
+        def copy_x(i):
+            bank = held.pop(("x bank", i))
+            grouped = stage.tile([P, BANK], F32, name="x_grouped", align_bytes=64)
+            nc.scalar.copy(
+                out=grouped[:].rearrange("p (g r u) -> p g r u", g=W_PASSES, r=P, u=2),
+                in_=bank[:].rearrange("p (g u r) -> p g r u", g=W_PASSES, u=2, r=P),
             )
-            live[("xg", i)] = xg
+            held[("x grouped", i)] = grouped
 
-        def qzx(i):
-            xg = live.pop(("xg", i))
+        def quantise_x(i):
+            grouped = held.pop(("x grouped", i))
             nc.vector.quantize_mx(
-                out=xq[:, i, :].bitcast(FP8X4), scales=xs[:, i, :], in_=xg[:].bitcast(BF16),
+                out=x_codes[:, i, :].bitcast(FP8X4), scales=x_scales[:, i, :], in_=grouped[:].bitcast(BF16),
             )
 
-        def tk(i, h):
-            tp = tpool.tile([P, 512], F32, name="tp")
-            for s in range(4):
-                base = i * 1024 + h * 512 + s * P
-                nc.tensor.transpose(
-                    out=tp[:, s * P:(s + 1) * P], in_=kw[:, base: base + P], identity=ident[:],
+        def transpose_k(j):
+            for h in range(2):
+                held[("k bank", j, h)] = transpose_words(k_words, (2 * j + h) * BANK)
+
+        def copy_k(j):
+            grouped = stage.tile([P, 2 * BANK], F32, name="k_grouped", align_bytes=64)
+            for h in range(2):
+                bank = held.pop(("k bank", j, h))
+                nc.scalar.copy(
+                    out=grouped[:].rearrange("p (r h s) -> p h r s", h=2, s=BANK // P)[:, h],
+                    in_=bank[:].rearrange("p (s r) -> p r s", s=BANK // P),
                 )
-            live[("tk", i, h)] = tp
+            held[("k grouped", j)] = grouped
 
-        def ek(i, h, eng):
-            if ("kg", i) not in live:
-                kg_new = stage.tile([P, 1024], F32, name="kg", align_bytes=64)
-                live[("kg", i)] = kg_new
-            kg = live[("kg", i)]
-            tp = live.pop(("tk", i, h))
-            copy_out(
-                eng,
-                kg[:].rearrange("p (r h s) -> p h r s", h=2, s=4)[:, h],
-                tp[:].rearrange("p (s r) -> p r s", s=4),
-            )
-
-        def qzk(i):
-            kg = live.pop(("kg", i))
+        def quantise_k(j):
+            grouped = held.pop(("k grouped", j))
             nc.vector.quantize_mx(
-                out=kq[:, i, :].bitcast(FP8X4), scales=ks[:, i, :], in_=kg[:].bitcast(BF16),
+                out=k_codes[:, j, :].bitcast(FP8X4), scales=k_scales[:, j, :], in_=grouped[:].bitcast(BF16),
             )
 
-        def m1(i):
-            qp = tpool.tile([P, 512], F32, name="tp")
-            for t in range(4):
-                for g in range(2):
+
+        def queries(i):
+            bank = psum.tile([P, BANK], F32, name="bank")
+            for t in range(Q_BLOCKS):
+                for g in range(W_PASSES):
                     nc.tensor.matmul_mx(
-                        out=qp[:, t * P:(t + 1) * P],
-                        lhsT=wq[:, g, t * P:(t + 1) * P].bitcast(FP8X4),
-                        lhsT_scale=ws[:, g, t * P:(t + 1) * P],
-                        rhs=xq[:, i, g * P:(g + 1) * P].bitcast(FP8X4),
-                        rhs_scale=xs[:, i, g * P:(g + 1) * P],
-                        start=(g == 0), stop=(g == 1),
+                        out=bank[:, t * P:(t + 1) * P],
+                        lhsT=w_codes[:, g, t * P:(t + 1) * P].bitcast(FP8X4),
+                        lhsT_scale=w_scales[:, g, t * P:(t + 1) * P],
+                        rhs=x_codes[:, i, g * P:(g + 1) * P].bitcast(FP8X4),
+                        rhs_scale=x_scales[:, i, g * P:(g + 1) * P],
+                        start=(g == 0), stop=(g == W_PASSES - 1),
                     )
-            live[("qp", i)] = qp
+            held[("q bank", i)] = bank
 
-        def badd(i):
-            qp = live.pop(("qp", i))
-            qg = stage.tile([P, 512], BF16, name="qg", align_bytes=64)
+        def add_bias(i):
+            bank = held.pop(("q bank", i))
+            grouped = stage.tile([P, BANK], BF16, name="q_grouped", align_bytes=64)
             nc.vector.tensor_tensor(
-                out=qg[:].rearrange("p (r t) -> p r t", t=4),
-                in0=qp[:].rearrange("p (t r) -> p r t", t=4),
-                in1=bias[:].unsqueeze(1).to_broadcast([P, P, 4]),
+                out=grouped[:].rearrange("p (r t) -> p r t", t=Q_BLOCKS),
+                in0=bank[:].rearrange("p (t r) -> p r t", t=Q_BLOCKS),
+                in1=bias[:].unsqueeze(1).to_broadcast([P, P, Q_BLOCKS]),
                 op=ALU.add,
             )
-            live[("qg", i)] = qg
+            held[("q grouped", i)] = grouped
 
-        def qzq(i):
-            qg = live.pop(("qg", i))
+        def quantise_q(i):
+            grouped = held.pop(("q grouped", i))
             nc.vector.quantize_mx(
-                out=qq[:, i, :].bitcast(FP8X4), scales=qs[:, i, :], in_=qg[:],
+                out=q_codes[:, i, :].bitcast(FP8X4), scales=q_scales[:, i, :], in_=grouped[:],
             )
 
-        def m2(i, c):
-            b = i // 2
-            sp = tpool.tile([P, 512], F32, name="tp")
-            nc.tensor.matmul_mx(
-                out=sp[:],
-                lhsT=qq[:, i, :].bitcast(FP8X4), lhsT_scale=qs[:, i, :],
-                rhs=kq[:, 2 * b + c, :].bitcast(FP8X4), rhs_scale=ks[:, 2 * b + c, :],
-                start=True, stop=True,
-            )
-            live[("sp", i, c)] = sp
 
-        def mx(i, c):
-            if ("nm", i) not in live:
-                nm_new = small.tile([P, 2], F32, name="nm")
-                live[("nm", i)] = nm_new
-            nm = live[("nm", i)]
-            nc.vector.tensor_reduce(
-                out=nm[:, c:c + 1], in_=live[("sp", i, c)][:], axis=AX.X, op=ALU.max, negate=True,
-            )
+        def scores(i):
+            for c in range(HALVES_A_BATCH):
+                bank = psum.tile([P, BANK], F32, name="bank")
+                j = HALVES_A_BATCH * (i // TILES_A_BATCH) + c
+                nc.tensor.matmul_mx(
+                    out=bank[:],
+                    lhsT=q_codes[:, i, :].bitcast(FP8X4), lhsT_scale=q_scales[:, i, :],
+                    rhs=k_codes[:, j, :].bitcast(FP8X4), rhs_scale=k_scales[:, j, :],
+                    start=True, stop=True,
+                )
+                held[("scores", i, c)] = bank
 
-        def nmx(i):
-            nm = live.pop(("nm", i))
-            nmn = small.tile([P, 1], F32, name="nmn")
-            nc.vector.tensor_tensor(out=nmn[:], in0=nm[:, 0:1], in1=nm[:, 1:2], op=ALU.min)
-            live[("nmn", i)] = nmn
+        def negated_maximum(i):
+            bank_maxima = small.tile([P, HALVES_A_BATCH], F32, name="bank_maxima")
+            for c in range(HALVES_A_BATCH):
+                nc.vector.tensor_reduce(
+                    out=bank_maxima[:, c:c + 1], in_=held[("scores", i, c)][:], axis=AX.X, op=ALU.max, negate=True,
+                )
+            shift = small.tile([P, 1], F32, name="shift")
+            nc.vector.tensor_tensor(out=shift[:], in0=bank_maxima[:, 0:1], in1=bank_maxima[:, 1:2], op=ALU.min)
+            held[("shift", i)] = shift
 
-        def expo(i, c):
-            if c == 0:
-                ee_new = stage.tile([P, 1024], F32, name="ee", bufs=4)
-                sm_new = small.tile([P, 2], F32, name="sm")
-                live[("ee", i)] = ee_new
-                live[("sm", i)] = sm_new
-            ee = live[("ee", i)]
-            sm = live[("sm", i)]
-            sp = live.pop(("sp", i, c))
+        def exponentials(i):
+            weights = stage.tile([P, PIXELS], F32, name="weights", bufs=4)
+            bank_sums = small.tile([P, HALVES_A_BATCH], F32, name="bank_sums")
+            for c in range(HALVES_A_BATCH):
+                nc.scalar.activation(
+                    out=weights[:, c * BANK:(c + 1) * BANK], in_=held.pop(("scores", i, c))[:], func=ACT.Exp,
+                    bias=held[("shift", i)][:, 0:1], scale=1.0, accum_out=bank_sums[:, c:c + 1],
+                )
+            held[("weights", i)] = weights
+            held[("bank sums", i)] = bank_sums
+
+        def row_sum(i):
+            bank_sums = held.pop(("bank sums", i))
+            total = small.tile([P, 1], F32, name="total")
             nc.scalar.activation(
-                out=ee[:, c * 512:(c + 1) * 512], in_=sp[:], func=ACT.Exp,
-                bias=live[("nmn", i)][:, 0:1], scale=1.0, accum_out=sm[:, c:c + 1],
+                out=total[:], in_=bank_sums[:, 0:1], func=ACT.Identity, bias=bank_sums[:, 1:2], scale=1.0,
             )
+            held[("total", i)] = total
 
-        def tot(i):
-            sm = live.pop(("sm", i))
-            tt = small.tile([P, 1], F32, name="tt")
-            nc.scalar.activation(out=tt[:], in_=sm[:, 0:1], func=ACT.Identity, bias=sm[:, 1:2], scale=1.0)
-            live[("tt", i)] = tt
+        def finish(i, pieces):
+            inverse = small.tile([P, 1], F32, name="inverse")
+            nc.vector.reciprocal(out=inverse[:], in_=held.pop(("total", i))[:])
+            weights = held.pop(("weights", i))
+            result = stage.tile([P, PIXELS], F32, name="result")
+            width = PIXELS // pieces
+            for lo in range(0, PIXELS, width):
+                nc.vector.scalar_tensor_tensor(
+                    out=result[:, lo:lo + width], in0=weights[:, lo:lo + width], scalar=inverse[:, 0:1],
+                    in1=mask_raw[:, i * PIXELS + lo: i * PIXELS + lo + width], op0=ALU.mult, op1=ALU.mult,
+                )
+                nc.sync.dma_start(
+                    out=out[i // TILES_A_BATCH].rearrange("(r a) y -> r a y", a=TILES_A_BATCH)[
+                        :, i % TILES_A_BATCH, lo:lo + width],
+                    in_=result[:, lo:lo + width],
+                )
 
-        def rs(i):
-            tt = live.pop(("tt", i))
-            rr = small.tile([P, 1], F32, name="rr")
-            nc.vector.reciprocal(out=rr[:], in_=tt[:])
-            live[("rr", i)] = rr
 
-        def fin(i, lo=0, hi=1024):
-            if lo == 0:
-                oo_new = stage.tile([P, 1024], F32, name="oo")
-                live[("oo", i)] = oo_new
-            nc.vector.scalar_tensor_tensor(
-                out=live[("oo", i)][:, lo:hi], in0=live[("ee", i)][:, lo:hi], scalar=live[("rr", i)][:, 0:1],
-                in1=mraw[:, i * 1024 + lo: i * 1024 + hi], op0=ALU.mult, op1=ALU.mult,
-            )
+        for g in range(W_PASSES):
+            load_w(g)
+        load_x(0)
+        load_bias()
+        for b in range(1, BATCH):
+            load_x(b)
+        for j in range(N_HALVES):
+            load_k(j)
+        for b in range(BATCH):
+            load_mask(b)
 
-        def st(i, lo=0, hi=1024):
-            nc.sync.dma_start(
-                out=out[i // 2].rearrange("(r a) m -> r a m", a=2)[:, i % 2, lo:hi],
-                in_=live[("oo", i)][:, lo:hi],
-            )
+        warm_up()
+        for g in range(W_PASSES):
+            group_w(g, 0, "vector")
+            group_w(g, 1, "scalar")
+        for g in range(W_PASSES):
+            quantise_w(g)
 
-        ld_w(0)
-        ld_w(1)
-        ld_x(0)
-        with nc.allow_non_contiguous_dma(reason="bias: 256 pieces of 4 bytes, once"):
-            nc.sync.dma_start(
-                out=bias[:].rearrange("p (u e) -> p u e", u=2),
-                in_=bq.rearrange("(u p e) -> p u e", u=2, p=P, e=2),
-            )
-        ld_x(1)
-        ld_x(2)
-        ld_k(0)
-        ld_k(1)
-        ld_k(2)
-        ld_k(3)
-        ld_k(4)
-        ld_k(5)
-        ld_m(0)
-        ld_m(1)
-        ld_m(2)
-        dummy = tpool.tile([P, 512], F32, name="tp")
-        for rep in range(4):
-            nc.tensor.matmul(out=dummy[:], lhsT=wraw[:, 0:P], rhs=wraw[:, 0:512], start=True, stop=True)
-        wreg(0, 0, "V")
-        wreg(0, 1, "S")
-        wreg(1, 0, "V")
-        wreg(1, 1, "S")
-        qzw(0)
-        tx(0)
-        tx(1)
-        qzw(1)
-        ex(0, "S")
-        ex(1, "S")
-        tx(2)
-        qzx(0)
-        tx(3)
-        ex(2, "S")
-        qzx(1)
-        m1(0)
-        m1(1)
-        ex(3, "S")
-        qzx(2)
-        tx(4)
-        badd(0)
-        tx(5)
-        tk(0, 0)
-        tk(0, 1)
-        ex(4, "S")
-        qzx(3)
-        ex(5, "S")
-        m1(2)
-        m1(3)
-        badd(1)
-        qzq(0)
-        qzx(4)
-        ek(0, 0, "S")
-        badd(2)
-        ek(0, 1, "S")
-        qzq(1)
-        qzx(5)
-        tk(1, 0)
-        tk(1, 1)
-        tk(2, 0)
-        tk(2, 1)
-        badd(3)
-        ek(1, 0, "S")
-        m1(4)
-        m1(5)
-        qzq(2)
-        qzk(0)
-        ek(1, 1, "S")
-        badd(4)
-        qzq(3)
-        qzk(1)
-        ek(2, 0, "S")
-        m2(0, 0)
-        badd(5)
-        ek(2, 1, "S")
-        m2(0, 1)
-        m2(1, 0)
-        qzq(4)
-        qzq(5)
-        m2(1, 1)
-        mx(0, 0)
-        tk(3, 0)
-        mx(0, 1)
-        tk(3, 1)
-        tk(4, 0)
-        nmx(0)
-        qzk(2)
-        tk(4, 1)
-        expo(0, 0)
-        mx(1, 0)
-        expo(0, 1)
-        m2(2, 0)
-        mx(1, 1)
-        ek(3, 0, "S")
-        nmx(1)
-        tot(0)
-        rs(0)
-        fin(0)
-        ek(3, 1, "S")
-        expo(1, 0)
-        qzk(3)
-        expo(1, 1)
-        st(0)
-        mx(2, 0)
-        ek(4, 0, "S")
-        m2(2, 1)
-        m2(3, 0)
-        mx(2, 1)
-        ek(4, 1, "S")
-        m2(3, 1)
-        tk(5, 0)
-        nmx(2)
-        tot(1)
-        rs(1)
-        expo(2, 0)
-        tk(5, 1)
-        fin(1)
-        expo(2, 1)
-        qzk(4)
-        ek(5, 0, "S")
-        st(1)
-        mx(3, 0)
-        ek(5, 1, "S")
-        m2(4, 0)
-        mx(3, 1)
-        nmx(3)
-        tot(2)
-        rs(2)
-        expo(3, 0)
-        fin(2)
-        expo(3, 1)
-        qzk(5)
-        st(2)
-        mx(4, 0)
-        m2(4, 1)
-        m2(5, 0)
-        mx(4, 1)
-        m2(5, 1)
-        nmx(4)
-        tot(3)
-        rs(3)
-        expo(4, 0)
-        fin(3)
-        expo(4, 1)
-        mx(5, 0)
-        st(3)
-        mx(5, 1)
-        nmx(5)
-        tot(4)
-        rs(4)
-        expo(5, 0)
-        fin(4)
-        expo(5, 1)
-        st(4)
-        tot(5)
-        rs(5)
-        fin(5, 0, 512)
-        st(5, 0, 512)
-        fin(5, 512, 1024)
-        st(5, 512, 1024)
+        loads = [("x", b) for b in range(BATCH)] + [("k", j) for j in range(N_HALVES)]
+        runs = [loads[first:first + 2] for first in range(0, len(loads), 2)]
+        between = [("x", i) for i in range(X_TILES_AHEAD, N_TILES)] + [("k", j) for j in range(HALVES_A_BATCH)]
+
+        def tiles_of(b):
+            return range(TILES_A_BATCH * b, TILES_A_BATCH * (b + 1))
+
+        def transposes(run):
+            for kind, index in run:
+                if kind == "x":
+                    for i in tiles_of(index):
+                        transpose_x(i)
+                else:
+                    transpose_k(index)
+
+        def copies(run):
+            for kind, index in run:
+                if kind == "x":
+                    for i in tiles_of(index):
+                        copy_x(i)
+                else:
+                    copy_k(index)
+
+        def bias_step(i):
+            add_bias(i)
+            if i > 0:
+                quantise_q(i - 1)
+            if i < len(between):
+                kind, index = between[i]
+                if kind == "x":
+                    quantise_x(index)
+                else:
+                    quantise_k(index)
+
+        def scores_of_batch(b):
+            for i in tiles_of(b):
+                scores(i)
+            if BATCH + b < len(runs):
+                transposes(runs[BATCH + b])
+
+        for b in range(BATCH):
+            transposes(runs[b])
+            copies(runs[b])
+            if b == 0:
+                for i in range(X_TILES_AHEAD):
+                    quantise_x(i)
+            else:
+                for i in tiles_of(b - 1):
+                    bias_step(i)
+            for i in tiles_of(b):
+                queries(i)
+        for i in tiles_of(BATCH - 1):
+            bias_step(i)
+        quantise_q(N_TILES - 1)
+        scores_of_batch(0)
+
+        for i in range(N_TILES):
+            negated_maximum(i)
+            if i > 0:
+                finish(i - 1, 1)
+            if i + 2 < N_HALVES:
+                quantise_k(i + 2)
+            exponentials(i)
+            if i + 3 < N_HALVES:
+                copy_k(i + 3)
+            row_sum(i)
+            if i % TILES_A_BATCH == TILES_A_BATCH - 1 and i + 1 < N_TILES:
+                scores_of_batch((i + 1) // TILES_A_BATCH)
+        finish(N_TILES - 1, 2)

@@ -211,6 +211,16 @@ def tile_text2imgca_pa_kernel(tc, x1, Wq, bq, k_img, masks, out):
                 )
                 held[("scores", i, c)] = bank
 
+        def keep_warm(count):
+            unread = psum.tile([P, BANK], F32, name="bank")
+            for repeat in range(count):
+                nc.tensor.matmul_mx(
+                    out=unread[:],
+                    lhsT=q_codes[:, 0, :].bitcast(FP8X4), lhsT_scale=q_scales[:, 0, :],
+                    rhs=k_codes[:, 0, :].bitcast(FP8X4), rhs_scale=k_scales[:, 0, :],
+                    start=True, stop=True,
+                )
+
         def negated_maximum(i):
             bank_maxima = small.tile([P, HALVES_A_BATCH], F32, name="bank_maxima")
             for c in range(HALVES_A_BATCH):
@@ -344,4 +354,6 @@ def tile_text2imgca_pa_kernel(tc, x1, Wq, bq, k_img, masks, out):
             row_sum(i)
             if i % TILES_A_BATCH == TILES_A_BATCH - 1 and i + 1 < N_TILES:
                 scores_of_batch((i + 1) // TILES_A_BATCH)
+            if i < N_TILES - 2:
+                keep_warm(3)
         finish(N_TILES - 1, 2)

from contextlib import ExitStack

import concourse.mybir as mybir
from concourse.masks import make_identity

F32 = mybir.dt.float32
BF16 = mybir.dt.bfloat16
U32 = mybir.dt.uint32
U8 = mybir.dt.uint8
FP8X4 = mybir.dt.float8_e4m3fn_x4
ALU = mybir.AluOpType
ACT = mybir.ActivationFunctionType
AX = mybir.AxisListType

P = 128
PACK = 4
K_PASS = PACK * P
BANK = 512
BATCH, TOKENS, D_TEXT, D_QK, PIXELS = 3, 256, 1024, 512, 1024
TILES_A_BATCH = TOKENS // P
N_TILES = BATCH * TILES_A_BATCH
HALVES_A_BATCH = PIXELS // BANK
N_HALVES = BATCH * HALVES_A_BATCH
W_PASSES = D_TEXT // K_PASS
Q_BLOCKS = D_QK // P
WARM_UP_MATMULS = 4
X_TILES_AHEAD = 3
FLOPS = 2 * BATCH * TOKENS * D_TEXT * D_QK + 2 * BATCH * TOKENS * PIXELS * D_QK


def tile_text2imgca_pa_kernel(tc, x1, Wq, bq, k_img, masks, out):
    nc = tc.nc
    with ExitStack() as ctx:
        keep = ctx.enter_context(tc.tile_pool(name="keep", bufs=1))
        stage = ctx.enter_context(tc.tile_pool(name="stage", bufs=3))
        small = ctx.enter_context(tc.tile_pool(name="small", bufs=4))
        psum = ctx.enter_context(tc.psum_pool(name="psum", bufs=8))

        identity = keep.tile([P, P], F32, name="identity")
        make_identity(nc, identity[:])

        w_raw = keep.tile([P, W_PASSES * PACK * D_QK], BF16, name="w_raw")
        w_grouped = keep.tile([P, W_PASSES * PACK * D_QK], BF16, name="w_grouped", align_bytes=64)
        w_codes = keep.tile([P, W_PASSES, D_QK], U32, name="w_codes", align_bytes=64)
        w_scales = keep.tile([P, W_PASSES, D_QK], U8, name="w_scales", align_bytes=64)
        x_raw = keep.tile([P, N_TILES * D_TEXT], BF16, name="x_raw")
        x_codes = keep.tile([P, N_TILES, W_PASSES * P], U32, name="x_codes", align_bytes=64)
        x_scales = keep.tile([P, N_TILES, W_PASSES * P], U8, name="x_scales", align_bytes=64)
        k_raw = keep.tile([P, N_HALVES * PACK * D_QK], BF16, name="k_raw")
        k_codes = keep.tile([P, N_HALVES, BANK], U32, name="k_codes", align_bytes=64)
        k_scales = keep.tile([P, N_HALVES, BANK], U8, name="k_scales", align_bytes=64)
        q_codes = keep.tile([P, N_TILES, P], U32, name="q_codes", align_bytes=64)
        q_scales = keep.tile([P, N_TILES, P], U8, name="q_scales", align_bytes=64)
        mask_raw = keep.tile([P, N_TILES * PIXELS], BF16, name="mask_raw")
        bias = keep.tile([P, Q_BLOCKS], BF16, name="bias")
        exp_in = keep.tile([P, 1], F32, name="exp_in")
        exp_out = keep.tile([P, 1], F32, name="exp_out")

        nc.vector.memset(exp_in[:], 0.0)
        nc.scalar.activation(out=exp_out[:], in_=exp_in[:], func=ACT.Exp)


        def load_w(g):
            nc.sync.dma_start(
                out=w_raw[:, g * PACK * D_QK:(g + 1) * PACK * D_QK].rearrange("p (u f) -> p u f", u=2),
                in_=Wq[g * K_PASS:(g + 1) * K_PASS, :].rearrange("(u p e) n -> p u (e n)", u=2, p=P, e=2),
            )

        def load_bias():
            with nc.allow_non_contiguous_dma(reason="bias: 256 pieces of 4 bytes, once"):
                nc.sync.dma_start(
                    out=bias[:].rearrange("p (u e) -> p u e", u=2),
                    in_=bq.rearrange("(u p e) -> p u e", u=2, p=P, e=2),
                )

        def load_x(b):
            nc.sync.dma_start(
                out=x_raw[:, b * TILES_A_BATCH * D_TEXT:(b + 1) * TILES_A_BATCH * D_TEXT],
                in_=x1[b].rearrange("(r a) k -> r (a k)", a=TILES_A_BATCH),
            )

        def load_k(j):
            first_pixel = (j % HALVES_A_BATCH) * BANK
            nc.sync.dma_start(
                out=k_raw[:, j * PACK * D_QK:(j + 1) * PACK * D_QK],
                in_=k_img[j // HALVES_A_BATCH, first_pixel:first_pixel + BANK, :].rearrange("(r a) d -> r (a d)", a=4),
            )

        def load_mask(b):
            nc.sync.dma_start(
                out=mask_raw[:, b * TILES_A_BATCH * PIXELS:(b + 1) * TILES_A_BATCH * PIXELS],
                in_=masks[b].rearrange("(r a) y -> r (a y)", a=TILES_A_BATCH),
            )

        x_words = x_raw[:].bitcast(F32)
        k_words = k_raw[:].bitcast(F32)
        held = {}


        w_in = w_raw[:].rearrange("p (g t u m e) -> p g t u m e", g=W_PASSES, t=PACK, u=2, m=P, e=2)
        w_out = w_grouped[:].rearrange("p (g u e m t) -> p g u e m t", g=W_PASSES, u=2, e=2, m=P, t=PACK)

        def group_w(g, e, engine):
            source = w_in[:, g, :, :, :, e].rearrange("p t u m -> p u m t")
            if engine == "vector":
                nc.vector.tensor_copy(out=w_out[:, g, :, e], in_=source)
            else:
                nc.scalar.copy(out=w_out[:, g, :, e], in_=source)

        def quantise_w(g):
            nc.vector.quantize_mx(
                out=w_codes[:, g, :].bitcast(FP8X4), scales=w_scales[:, g, :],
                in_=w_grouped[:, g * PACK * D_QK:(g + 1) * PACK * D_QK],
            )

        def warm_up():
            unread = psum.tile([P, BANK], F32, name="bank")
            for repeat in range(WARM_UP_MATMULS):
                nc.tensor.matmul(out=unread[:], lhsT=w_raw[:, 0:P], rhs=w_raw[:, 0:BANK], start=True, stop=True)


        def transpose_words(words, first):
            bank = psum.tile([P, BANK], F32, name="bank")
            for s in range(BANK // P):
                nc.tensor.transpose(
                    out=bank[:, s * P:(s + 1) * P], in_=words[:, first + s * P: first + (s + 1) * P],
                    identity=identity[:],
                )
            return bank

        def transpose_x(i):
            held[("x bank", i)] = transpose_words(x_words, i * BANK)

        def copy_x(i):
            bank = held.pop(("x bank", i))
            grouped = stage.tile([P, BANK], F32, name="x_grouped", align_bytes=64)
            nc.scalar.copy(
                out=grouped[:].rearrange("p (g r u) -> p g r u", g=W_PASSES, r=P, u=2),
                in_=bank[:].rearrange("p (g u r) -> p g r u", g=W_PASSES, u=2, r=P),
            )
            held[("x grouped", i)] = grouped

        def quantise_x(i):
            grouped = held.pop(("x grouped", i))
            nc.vector.quantize_mx(
                out=x_codes[:, i, :].bitcast(FP8X4), scales=x_scales[:, i, :], in_=grouped[:].bitcast(BF16),
            )

        def transpose_k(j):
            for h in range(2):
                held[("k bank", j, h)] = transpose_words(k_words, (2 * j + h) * BANK)

        def copy_k(j):
            grouped = stage.tile([P, 2 * BANK], F32, name="k_grouped", align_bytes=64)
            for h in range(2):
                bank = held.pop(("k bank", j, h))
                nc.scalar.copy(
                    out=grouped[:].rearrange("p (r h s) -> p h r s", h=2, s=BANK // P)[:, h],
                    in_=bank[:].rearrange("p (s r) -> p r s", s=BANK // P),
                )
            held[("k grouped", j)] = grouped

        def quantise_k(j):
            grouped = held.pop(("k grouped", j))
            nc.vector.quantize_mx(
                out=k_codes[:, j, :].bitcast(FP8X4), scales=k_scales[:, j, :], in_=grouped[:].bitcast(BF16),
            )


        def queries(i):
            bank = psum.tile([P, BANK], F32, name="bank")
            for t in range(Q_BLOCKS):
                for g in range(W_PASSES):
                    nc.tensor.matmul_mx(
                        out=bank[:, t * P:(t + 1) * P],
                        lhsT=w_codes[:, g, t * P:(t + 1) * P].bitcast(FP8X4),
                        lhsT_scale=w_scales[:, g, t * P:(t + 1) * P],
                        rhs=x_codes[:, i, g * P:(g + 1) * P].bitcast(FP8X4),
                        rhs_scale=x_scales[:, i, g * P:(g + 1) * P],
                        start=(g == 0), stop=(g == W_PASSES - 1),
                    )
            held[("q bank", i)] = bank

        def add_bias(i):
            bank = held.pop(("q bank", i))
            grouped = stage.tile([P, BANK], BF16, name="q_grouped", align_bytes=64)
            nc.vector.tensor_tensor(
                out=grouped[:].rearrange("p (r t) -> p r t", t=Q_BLOCKS),
                in0=bank[:].rearrange("p (t r) -> p r t", t=Q_BLOCKS),
                in1=bias[:].unsqueeze(1).to_broadcast([P, P, Q_BLOCKS]),
                op=ALU.add,
            )
            held[("q grouped", i)] = grouped

        def quantise_q(i):
            grouped = held.pop(("q grouped", i))
            nc.vector.quantize_mx(
                out=q_codes[:, i, :].bitcast(FP8X4), scales=q_scales[:, i, :], in_=grouped[:],
            )


        def scores(i):
            for c in range(HALVES_A_BATCH):
                bank = psum.tile([P, BANK], F32, name="bank")
                j = HALVES_A_BATCH * (i // TILES_A_BATCH) + c
                nc.tensor.matmul_mx(
                    out=bank[:],
                    lhsT=q_codes[:, i, :].bitcast(FP8X4), lhsT_scale=q_scales[:, i, :],
                    rhs=k_codes[:, j, :].bitcast(FP8X4), rhs_scale=k_scales[:, j, :],
                    start=True, stop=True,
                )
                held[("scores", i, c)] = bank

        def keep_warm(count):
            unread = psum.tile([P, BANK], F32, name="bank")
            for repeat in range(count):
                nc.tensor.matmul_mx(
                    out=unread[:],
                    lhsT=q_codes[:, 0, :].bitcast(FP8X4), lhsT_scale=q_scales[:, 0, :],
                    rhs=k_codes[:, 0, :].bitcast(FP8X4), rhs_scale=k_scales[:, 0, :],
                    start=True, stop=True,
                )

        def negated_maximum(i):
            bank_maxima = small.tile([P, HALVES_A_BATCH], F32, name="bank_maxima")
            for c in range(HALVES_A_BATCH):
                nc.vector.tensor_reduce(
                    out=bank_maxima[:, c:c + 1], in_=held[("scores", i, c)][:], axis=AX.X, op=ALU.max, negate=True,
                )
            shift = small.tile([P, 1], F32, name="shift")
            nc.vector.tensor_tensor(out=shift[:], in0=bank_maxima[:, 0:1], in1=bank_maxima[:, 1:2], op=ALU.min)
            held[("shift", i)] = shift

        def exponentials(i):
            weights = stage.tile([P, PIXELS], F32, name="weights", bufs=4)
            bank_sums = small.tile([P, HALVES_A_BATCH], F32, name="bank_sums")
            for c in range(HALVES_A_BATCH):
                nc.scalar.activation(
                    out=weights[:, c * BANK:(c + 1) * BANK], in_=held.pop(("scores", i, c))[:], func=ACT.Exp,
                    bias=held[("shift", i)][:, 0:1], scale=1.0, accum_out=bank_sums[:, c:c + 1],
                )
            held[("weights", i)] = weights
            held[("bank sums", i)] = bank_sums

        def row_sum(i):
            bank_sums = held.pop(("bank sums", i))
            total = small.tile([P, 1], F32, name="total")
            nc.scalar.activation(
                out=total[:], in_=bank_sums[:, 0:1], func=ACT.Identity, bias=bank_sums[:, 1:2], scale=1.0,
            )
            held[("total", i)] = total

        def finish(i, pieces):
            inverse = small.tile([P, 1], F32, name="inverse")
            nc.vector.reciprocal(out=inverse[:], in_=held.pop(("total", i))[:])
            weights = held.pop(("weights", i))
            result = stage.tile([P, PIXELS], F32, name="result")
            width = PIXELS // pieces
            for lo in range(0, PIXELS, width):
                nc.vector.scalar_tensor_tensor(
                    out=result[:, lo:lo + width], in0=weights[:, lo:lo + width], scalar=inverse[:, 0:1],
                    in1=mask_raw[:, i * PIXELS + lo: i * PIXELS + lo + width], op0=ALU.mult, op1=ALU.mult,
                )
                nc.sync.dma_start(
                    out=out[i // TILES_A_BATCH].rearrange("(r a) y -> r a y", a=TILES_A_BATCH)[
                        :, i % TILES_A_BATCH, lo:lo + width],
                    in_=result[:, lo:lo + width],
                )


        for g in range(W_PASSES):
            load_w(g)
        load_x(0)
        load_bias()
        for b in range(1, BATCH):
            load_x(b)
        for j in range(N_HALVES):
            load_k(j)
        for b in range(BATCH):
            load_mask(b)

        warm_up()
        for g in range(W_PASSES):
            group_w(g, 0, "vector")
            group_w(g, 1, "scalar")
        for g in range(W_PASSES):
            quantise_w(g)

        loads = [("x", b) for b in range(BATCH)] + [("k", j) for j in range(N_HALVES)]
        runs = [loads[first:first + 2] for first in range(0, len(loads), 2)]
        between = [("x", i) for i in range(X_TILES_AHEAD, N_TILES)] + [("k", j) for j in range(HALVES_A_BATCH)]

        def tiles_of(b):
            return range(TILES_A_BATCH * b, TILES_A_BATCH * (b + 1))

        def transposes(run):
            for kind, index in run:
                if kind == "x":
                    for i in tiles_of(index):
                        transpose_x(i)
                else:
                    transpose_k(index)

        def copies(run):
            for kind, index in run:
                if kind == "x":
                    for i in tiles_of(index):
                        copy_x(i)
                else:
                    copy_k(index)

        def bias_step(i):
            add_bias(i)
            if i > 0:
                quantise_q(i - 1)
            if i < len(between):
                kind, index = between[i]
                if kind == "x":
                    quantise_x(index)
                else:
                    quantise_k(index)

        def scores_of_batch(b):
            for i in tiles_of(b):
                scores(i)
            if BATCH + b < len(runs):
                transposes(runs[BATCH + b])

        for b in range(BATCH):
            transposes(runs[b])
            copies(runs[b])
            if b == 0:
                for i in range(X_TILES_AHEAD):
                    quantise_x(i)
            else:
                for i in tiles_of(b - 1):
                    bias_step(i)
            for i in tiles_of(b):
                queries(i)
        for i in tiles_of(BATCH - 1):
            bias_step(i)
        quantise_q(N_TILES - 1)
        scores_of_batch(0)

        for i in range(N_TILES):
            negated_maximum(i)
            if i > 0:
                finish(i - 1, 1)
            if i + 2 < N_HALVES:
                quantise_k(i + 2)
            exponentials(i)
            if i + 3 < N_HALVES:
                copy_k(i + 3)
            row_sum(i)
            if i % TILES_A_BATCH == TILES_A_BATCH - 1 and i + 1 < N_TILES:
                scores_of_batch((i + 1) // TILES_A_BATCH)
            if i < N_TILES - 2:
                keep_warm(3)
        finish(N_TILES - 1, 2)
